import numpy as np
import ml_dtypes


def mxq(x, axis, fmt="e4m3"):
    dtype, down = {"e4m3": (ml_dtypes.float8_e4m3fn, 7), "e5m2": (ml_dtypes.float8_e5m2, 14)}[fmt]
    v = np.moveaxis(np.asarray(x, np.float32).astype(ml_dtypes.bfloat16).astype(np.float64), axis, -1)
    blocks = v.reshape(v.shape[:-1] + (-1, 32))
    amax = np.abs(blocks).max(-1, keepdims=True)
    byte = np.maximum(np.where(amax > 0, np.frexp(amax)[1] - 1 + 127, 0) - down, 1)
    scale = np.exp2(byte - 127.0)
    codes = (blocks / scale).astype(np.float32).astype(dtype).astype(np.float64)
    return np.moveaxis((codes * scale).reshape(v.shape), -1, axis)


WIDE = False


def mx_kscale(k):
    if not WIDE:
        return np.ones(k)
    levels = np.array([10, -10, 5, -5, 0])
    if k % 512:
        return np.exp2(np.random.permutation(np.resize(levels, k // 32))).repeat(32)
    a = np.empty((k // 512, 16))
    for p in range(k // 512):
        a[p, :8] = np.random.permutation(np.resize(levels, 8))
        for g in range(8):
            far = levels[np.abs(levels - a[p, g]) >= 10]
            a[p, g + 8] = far[np.random.randint(len(far))]
    return np.exp2(a.ravel()).repeat(32)


BF16 = ml_dtypes.bfloat16


def bf(x):
    return np.asarray(x, np.float32).astype(BF16)


def f64(x):
    return np.asarray(x).astype(np.float64)


N, C, I = 512, 128, 8
EPS = 1e-5


def sigmoid(v):
    return 1.0 / (1.0 + np.exp(-v))


def layernorm(x, g, b):
    mu = x.mean(-1, keepdims=True)
    var = np.square(x - mu).mean(-1, keepdims=True)
    return (x - mu) / np.sqrt(var + EPS) * g + b


def setup_inputs():
    s = mx_kscale(N)[None, :, None]
    return {"left_proj": bf(np.random.standard_normal((N, N, I)) * s),
            "left_gate": bf(np.random.standard_normal((N, N, I))),
            "right_proj": bf(np.random.standard_normal((N, N, I)) / s),
            "right_gate": bf(np.random.standard_normal((N, N, I))),
            "mask": bf(np.random.uniform(size=(N, N)) > 0.5),
            "ln_c_g": bf(1.0 + 0.1 * np.random.standard_normal(I)),
            "ln_c_b": bf(0.1 * np.random.standard_normal(I))}


def reference(left_proj, left_gate, right_proj, right_gate, mask, ln_c_g, ln_c_b):
    m = f64(mask)[..., None]
    left = m * f64(left_proj) * sigmoid(f64(left_gate))
    right = m * f64(right_proj) * sigmoid(f64(right_gate))
    lt = left.transpose(2, 0, 1)
    rt = right.transpose(2, 1, 0)
    x = (mxq(lt, 2, "e4m3") @ mxq(rt, 1, "e4m3")).transpose(1, 2, 0)
    return layernorm(x, f64(ln_c_g), f64(ln_c_b))

@@ -1,0 +1,286 @@
+from contextlib import ExitStack
+
+import concourse.mybir as mybir
+from concourse.masks import make_identity
+
+BF16 = mybir.dt.bfloat16
+F32 = mybir.dt.float32
+U32 = mybir.dt.uint32
+U8 = mybir.dt.uint8
+FP8X4 = mybir.dt.float8_e4m3fn_x4
+ACT = mybir.ActivationFunctionType
+ALU = mybir.AluOpType
+
+P = 128
+PACK = 4
+RES = 512
+CH = 8
+PAIRS = CH // 2
+TILES = RES // P
+HALF = RES // 2
+QUAD = 4
+LEAD = 2
+SIG_LEAD = 3
+BANKS = 6
+EPS = 1e-5
+
+FLOPS = 2 * RES * RES * RES * CH
+
+
+def tile_net2_pa_kernel(
+    tc, left_proj, left_gate, right_proj, right_gate, mask, ln_c_g, ln_c_b, out
+):
+    nc = tc.nc
+    with ExitStack() as ctx:
+        ctx.enter_context(tc.manual_schedule())
+        keep = ctx.enter_context(tc.tile_pool(name="keep", bufs=1))
+        psum = ctx.enter_context(tc.psum_pool(name="psum", bufs=1))
+
+        ident_f32 = keep.tile([P, P], F32)
+        make_identity(nc, ident_f32)
+        ident_bf16 = keep.tile([P, P], BF16)
+        make_identity(nc, ident_bf16)
+
+        gain_bf16 = keep.tile([P, CH], BF16)
+        nc.scalar.dma_start(out=gain_bf16, in_=ln_c_g.partition_broadcast(P))
+        bias_bf16 = keep.tile([P, CH], BF16)
+        nc.scalar.dma_start(out=bias_bf16, in_=ln_c_b.partition_broadcast(P))
+        gain = keep.tile([P, CH], F32)
+        nc.vector.tensor_copy(out=gain, in_=gain_bf16)
+        bias = keep.tile([P, CH], F32)
+        nc.vector.tensor_copy(out=bias, in_=bias_bf16)
+        eps = keep.tile([P, 1], F32)
+        nc.vector.memset(eps, EPS)
+
+        left_codes = keep.tile([P, CH, RES], U32, align_bytes=64)
+        left_scales = keep.tile([P, CH, RES], U8, align_bytes=64)
+        right_codes = keep.tile([P, CH, RES], U32, align_bytes=64)
+        right_scales = keep.tile([P, CH, RES], U8, align_bytes=64)
+        mask_kt = keep.tile([P, TILES, P, PACK], BF16)
+        means = keep.tile([P, TILES, RES], F32)
+
+        def product_pass(acc, a, c, start, stop):
+            rows = slice(a * P, (a + 1) * P)
+            nc.tensor.matmul_mx(
+                out=acc,
+                lhsT=left_codes[:, c, rows].bitcast(FP8X4),
+                lhsT_scale=left_scales[:, c, rows],
+                rhs=right_codes[:, c, :].bitcast(FP8X4),
+                rhs_scale=right_scales[:, c, :],
+                start=start,
+                stop=stop,
+            )
+
+        def mean_rows(a):
+            total = psum.tile([P, RES], F32, tag="stat")
+            for c in range(CH):
+                product_pass(total, a, c, c == 0, c == CH - 1)
+            nc.scalar.activation(out=means[:, a, :], in_=total, func=ACT.Copy, scale=1.0 / CH)
+
+        work = ctx.enter_context(tc.tile_pool(name="work", bufs=3))
+        with tc.tile_pool(name="loads", bufs=3) as loads:
+            sides = (
+                (right_proj, right_gate, right_codes, right_scales),
+                (left_proj, left_gate, left_codes, left_scales),
+            )
+            groups = [(s, n, w) for s in range(2) for n in range(TILES) for w in range(PAIRS)]
+            mask_rows = loads.tile([P, TILES, RES], BF16, bufs=1)
+            loaded = {}
+            sigmoids = {}
+            transposed = {}
+            gated = {}
+            masked = {}
+
+            def load_rows(g):
+                s, n, w = groups[g]
+                for which in (1, 0):
+                    rows = loads.tile([P, RES * CH], BF16, tag="rows%d" % which)
+                    nc.sync.dma_start(
+                        out=rows, in_=sides[s][which][n * P : (n + 1) * P].rearrange("r k c -> r (k c)")
+                    )
+                    loaded[(which, s, n)] = rows
+
+            def transposed_pair(which, g):
+                s, n, w = groups[g]
+                words = loaded[(which, s, n)].bitcast(F32).rearrange("r (k w) -> r k w", w=PAIRS)
+                bank = psum.tile([P, PACK, P], F32, tag="bank", bufs=BANKS)
+                for t in range(PACK):
+                    nc.tensor.transpose(bank[:, t, :], words[:, t : RES : PACK, w], ident_f32)
+                return bank.bitcast(BF16).rearrange("p t (r e) -> p e r t", e=2)
+
+            def sigmoid_group(g):
+                sig = work.tile([P, 2, P, PACK], F32, tag="sig", bufs=SIG_LEAD + 2)
+                nc.scalar.activation(out=sig, in_=transposed_pair(1, g), func=ACT.Sigmoid)
+                sigmoids[g] = sig
+
+            def transpose_mask(n):
+                mask_t = psum.tile([P, PACK, P], BF16, tag="stat")
+                for t in range(PACK):
+                    nc.tensor.transpose(mask_t[:, t, :], mask_rows[:, n, t : RES : PACK], ident_bf16)
+                nc.scalar.copy(out=mask_kt[:, n], in_=mask_t.rearrange("p t r -> p r t"))
+
+            def prepare_sigmoid(g):
+                s, n, w = groups[g]
+                if w == 0:
+                    load_rows(g)
+                sigmoid_group(g)
+
+            def prepare_projection(g):
+                s, n, w = groups[g]
+                transposed[g] = transposed_pair(0, g)
+                if s == 0 and w == 0:
+                    transpose_mask(n)
+
+            def gate_group(g):
+                product = work.tile([P, 2, P, PACK], BF16, tag="product", bufs=2 * PAIRS)
+                nc.vector.tensor_tensor(out=product, in0=transposed[g], in1=sigmoids[g], op=ALU.mult)
+                gated[g] = product
+
+            def mask_group(g):
+                s, n, w = groups[g]
+                if w < PAIRS // 2:
+                    engine = nc.vector
+                    kept = work.tile([P, 2, P, PACK], BF16, tag="kept_vector", bufs=PAIRS, align_bytes=64)
+                else:
+                    engine = nc.gpsimd
+                    kept = work.tile([P, 2, P, PACK], BF16, tag="kept_gpsimd", bufs=PAIRS // 2, align_bytes=64)
+                engine.tensor_tensor(
+                    out=kept,
+                    in0=gated[g],
+                    in1=mask_kt[:, n].unsqueeze(1).to_broadcast([P, 2, P, PACK]),
+                    op=ALU.mult,
+                )
+                masked[g] = kept
+
+            def quantise_group(g):
+                s, n, w = groups[g]
+                rows = slice(n * P, (n + 1) * P)
+                for e in range(2):
+                    nc.vector.quantize_mx(
+                        out=sides[s][2][:, 2 * w + e, rows].bitcast(FP8X4),
+                        scales=sides[s][3][:, 2 * w + e, rows],
+                        in_=masked[g][:, e].rearrange("p r t -> p (r t)"),
+                    )
+
+            def quantise_tile(first):
+                for g in range(first, first + PAIRS):
+                    quantise_group(g)
+
+            def mean_of_tile(first):
+                s, n, w = groups[first]
+                if s == 1:
+                    mean_rows(n)
+
+            load_rows(0)
+            nc.sync.dma_start(out=mask_rows, in_=mask.rearrange("(n r) k -> r n k", r=P))
+            for g in range(LEAD):
+                sigmoid_group(g)
+            for g in range(LEAD):
+                transposed[g] = transposed_pair(0, g)
+            transpose_mask(0)
+            for g in range(LEAD, SIG_LEAD):
+                sigmoid_group(g)
+
+            for first in range(0, len(groups), PAIRS):
+                for g in range(first, first + PAIRS):
+                    if g + LEAD < len(groups):
+                        prepare_projection(g + LEAD)
+                    if g + SIG_LEAD < len(groups):
+                        prepare_sigmoid(g + SIG_LEAD)
+                    gate_group(g)
+                for g in range(first, first + PAIRS):
+                    mask_group(g)
+                if first >= PAIRS:
+                    quantise_tile(first - PAIRS)
+                if first >= 2 * PAIRS:
+                    mean_of_tile(first - 2 * PAIRS)
+
+        with tc.tile_pool(name="norm", bufs=2) as norm:
+            planes = {}
+            squares = {}
+            rstds_t = {}
+            rstds = {}
+
+            def centre_rows(a):
+                centred = norm.tile([P, CH, RES], F32, tag="centred", bufs=4)
+                squared = norm.tile([P, CH, RES], F32, tag="squared")
+                for c in range(CH):
+                    x = psum.tile([P, RES], F32, tag="bank", bufs=BANKS)
+                    product_pass(x, a, c, True, True)
+                    nc.vector.tensor_tensor(out=centred[:, c, :], in0=x, in1=means[:, a, :], op=ALU.subtract)
+                    if c % 2 == 1:
+                        nc.scalar.activation(
+                            out=squared[:, c - 1 : c + 1, :], in_=centred[:, c - 1 : c + 1, :], func=ACT.Square
+                        )
+                planes[a] = centred
+                squares[a] = squared
+
+            def variance_rows(a):
+                var_t = psum.tile([P, TILES, P], F32, tag="stat")
+                for b in range(TILES):
+                    for c in range(CH):
+                        nc.tensor.matmul(
+                            out=var_t[:, b, :],
+                            lhsT=squares[a][:, c, b * P : (b + 1) * P],
+                            rhs=ident_f32,
+                            is_transpose=True,
+                            start=(c == 0),
+                            stop=(c == CH - 1),
+                        )
+                rstd_t = norm.tile([P, TILES, P], F32, tag="rstd_t")
+                nc.scalar.activation(
+                    out=rstd_t, in_=var_t, func=ACT.Abs_reciprocal_sqrt, scale=1.0 / CH, bias=eps
+                )
+                rstds_t[a] = rstd_t
+
+            def rstd_rows(a):
+                rstd = psum.tile([P, TILES, P], F32, tag="rstd")
+                for b in range(TILES):
+                    nc.tensor.transpose(rstd[:, b, :], rstds_t[a][:, b, :], ident_f32)
+                rstds[a] = rstd.rearrange("p b j -> p (b j)")
+
+            def normalise_rows(a):
+                centred = planes[a]
+                for q in range(0, CH, QUAD):
+                    nc.vector.tensor_tensor(
+                        out=centred[:, q : q + QUAD, :],
+                        in0=centred[:, q : q + QUAD, :],
+                        in1=rstds[a].unsqueeze(1).to_broadcast([P, QUAD, RES]),
+                        op=ALU.mult,
+                    )
+                for c in range(CH):
+                    nc.vector.tensor_scalar(
+                        out=centred[:, c, :],
+                        in0=centred[:, c, :],
+                        scalar1=gain[:, c : c + 1],
+                        scalar2=bias[:, c : c + 1],
+                        op0=ALU.mult,
+                        op1=ALU.add,
+                    )
+                for h in range(RES // HALF):
+                    cols = slice(h * HALF, (h + 1) * HALF)
+                    result = norm.tile([P, HALF, CH], F32, tag="result", bufs=3)
+                    for q in range(0, CH, QUAD):
+                        nc.scalar.copy(
+                            out=result[:, :, q : q + QUAD],
+                            in_=centred[:, q : q + QUAD, cols].rearrange("p c j -> p j c"),
+                        )
+                    nc.sync.dma_start(
+                        out=out[a * P : (a + 1) * P, cols, :].rearrange("i j c -> i (j c)"),
+                        in_=result.rearrange("p j c -> p (j c)"),
+                    )
+
+            centre_rows(0)
+            quantise_tile(len(groups) - PAIRS)
+            mean_of_tile(len(groups) - 2 * PAIRS)
+            centre_rows(1)
+            variance_rows(0)
+            for a in range(TILES):
+                if a + 2 < TILES:
+                    centre_rows(a + 2)
+                if a + 3 < TILES:
+                    mean_rows(a + 3)
+                rstd_rows(a)
+                if a + 1 < TILES:
+                    variance_rows(a + 1)
+                normalise_rows(a)

@@ -78,6 +78,53 @@ def tile_net2_pa_kernel(
             nc.scalar.activation(out=means[:, a, :], in_=total, func=ACT.Copy, scale=1.0 / CH)
 
         work = ctx.enter_context(tc.tile_pool(name="work", bufs=3))
+        norm = ctx.enter_context(tc.tile_pool(name="norm", bufs=2))
+        planes = {}
+        squares = {}
+        rstds_t = {}
+        rstds = {}
+
+        def centre_rows(a, pool):
+            centred = pool.tile([P, CH, RES], F32, tag="centred", bufs=2)
+            squared = norm.tile([P, CH, RES], F32, tag="squared", bufs=2)
+            for c in range(CH):
+                x = psum.tile([P, RES], F32, tag="bank", bufs=BANKS)
+                product_pass(x, a, c, True, True)
+                nc.vector.tensor_tensor(out=centred[:, c, :], in0=x, in1=means[:, a, :], op=ALU.subtract)
+                if c % 2 == 1:
+                    nc.scalar.activation(
+                        out=squared[:, c - 1 : c + 1, :], in_=centred[:, c - 1 : c + 1, :], func=ACT.Square
+                    )
+            planes[a] = centred
+            squares[a] = squared
+
+        def variance_rows(a):
+            var_t = psum.tile([P, TILES, P], F32, tag="stat")
+            for b in range(TILES):
+                for c in range(CH):
+                    nc.tensor.matmul(
+                        out=var_t[:, b, :],
+                        lhsT=squares[a][:, c, b * P : (b + 1) * P],
+                        rhs=ident_f32,
+                        is_transpose=True,
+                        start=(c == 0),
+                        stop=(c == CH - 1),
+                    )
+            rstd_t = norm.tile([P, TILES, P], F32, tag="rstd_t")
+            nc.scalar.activation(
+                out=rstd_t, in_=var_t, func=ACT.Abs_reciprocal_sqrt, scale=1.0 / CH, bias=eps
+            )
+            rstds_t[a] = rstd_t
+
+        def rstd_rows(a):
+            if a == 0:
+                rstd = psum.tile([P, TILES, P], F32, tag="rstd")
+            else:
+                rstd = psum.tile([P, TILES, P], F32, tag="bank", bufs=BANKS)
+            for b in range(TILES):
+                nc.tensor.transpose(rstd[:, b, :], rstds_t[a][:, b, :], ident_f32)
+            rstds[a] = rstd.rearrange("p b j -> p (b j)")
+
         with tc.tile_pool(name="loads", bufs=3) as loads:
             sides = (
                 (right_proj, right_gate, right_codes, right_scales),
@@ -132,7 +179,7 @@ def tile_net2_pa_kernel(
                     transpose_mask(n)
 
             def gate_group(g):
-                product = work.tile([P, 2, P, PACK], BF16, tag="product", bufs=2 * PAIRS)
+                product = work.tile([P, 2, P, PACK], BF16, tag="product", bufs=6)
                 nc.vector.tensor_tensor(out=product, in0=transposed[g], in1=sigmoids[g], op=ALU.mult)
                 gated[g] = product
 
@@ -166,11 +213,6 @@ def tile_net2_pa_kernel(
                 for g in range(first, first + PAIRS):
                     quantise_group(g)
 
-            def mean_of_tile(first):
-                s, n, w = groups[first]
-                if s == 1:
-                    mean_rows(n)
-
             load_rows(0)
             nc.sync.dma_start(out=mask_rows, in_=mask.rearrange("(n r) k -> r n k", r=P))
             for g in range(LEAD):
@@ -181,106 +223,86 @@ def tile_net2_pa_kernel(
             for g in range(LEAD, SIG_LEAD):
                 sigmoid_group(g)
 
-            for first in range(0, len(groups), PAIRS):
+            for turn in range(2 * TILES):
+                first = turn * PAIRS
+                a = turn - TILES - 2
                 for g in range(first, first + PAIRS):
                     if g + LEAD < len(groups):
                         prepare_projection(g + LEAD)
                     if g + SIG_LEAD < len(groups):
                         prepare_sigmoid(g + SIG_LEAD)
                     gate_group(g)
+                    if g == first + 1 and a >= 0:
+                        mean_rows(a)
+                if a == 1:
+                    variance_rows(0)
                 for g in range(first, first + PAIRS):
                     mask_group(g)
-                if first >= PAIRS:
+                if turn >= 1:
                     quantise_tile(first - PAIRS)
-                if first >= 2 * PAIRS:
-                    mean_of_tile(first - 2 * PAIRS)
+                if a >= 0:
+                    centre_rows(a, norm)
+            rstd_rows(0)
 
-        with tc.tile_pool(name="norm", bufs=2) as norm:
-            planes = {}
-            squares = {}
-            rstds_t = {}
-            rstds = {}
+        with tc.tile_pool(name="late", bufs=2) as late:
 
-            def centre_rows(a):
-                centred = norm.tile([P, CH, RES], F32, tag="centred", bufs=4)
-                squared = norm.tile([P, CH, RES], F32, tag="squared")
-                for c in range(CH):
-                    x = psum.tile([P, RES], F32, tag="bank", bufs=BANKS)
-                    product_pass(x, a, c, True, True)
-                    nc.vector.tensor_tensor(out=centred[:, c, :], in0=x, in1=means[:, a, :], op=ALU.subtract)
-                    if c % 2 == 1:
-                        nc.scalar.activation(
-                            out=squared[:, c - 1 : c + 1, :], in_=centred[:, c - 1 : c + 1, :], func=ACT.Square
-                        )
-                planes[a] = centred
-                squares[a] = squared
-
-            def variance_rows(a):
-                var_t = psum.tile([P, TILES, P], F32, tag="stat")
-                for b in range(TILES):
-                    for c in range(CH):
-                        nc.tensor.matmul(
-                            out=var_t[:, b, :],
-                            lhsT=squares[a][:, c, b * P : (b + 1) * P],
-                            rhs=ident_f32,
-                            is_transpose=True,
-                            start=(c == 0),
-                            stop=(c == CH - 1),
-                        )
-                rstd_t = norm.tile([P, TILES, P], F32, tag="rstd_t")
-                nc.scalar.activation(
-                    out=rstd_t, in_=var_t, func=ACT.Abs_reciprocal_sqrt, scale=1.0 / CH, bias=eps
-                )
-                rstds_t[a] = rstd_t
-
-            def rstd_rows(a):
-                rstd = psum.tile([P, TILES, P], F32, tag="rstd")
-                for b in range(TILES):
-                    nc.tensor.transpose(rstd[:, b, :], rstds_t[a][:, b, :], ident_f32)
-                rstds[a] = rstd.rearrange("p b j -> p (b j)")
-
-            def normalise_rows(a):
+            def normalise_half(a, h, on_vector):
                 centred = planes[a]
-                for q in range(0, CH, QUAD):
-                    nc.vector.tensor_tensor(
-                        out=centred[:, q : q + QUAD, :],
-                        in0=centred[:, q : q + QUAD, :],
-                        in1=rstds[a].unsqueeze(1).to_broadcast([P, QUAD, RES]),
-                        op=ALU.mult,
-                    )
+                cols = slice(h * HALF, (h + 1) * HALF)
+                nc.vector.tensor_tensor(
+                    out=centred[:, :, cols],
+                    in0=centred[:, :, cols],
+                    in1=rstds[a][:, cols].unsqueeze(1).to_broadcast([P, CH, HALF]),
+                    op=ALU.mult,
+                )
                 for c in range(CH):
-                    nc.vector.tensor_scalar(
-                        out=centred[:, c, :],
-                        in0=centred[:, c, :],
+                    engine = nc.vector if c < on_vector else nc.gpsimd
+                    engine.tensor_scalar(
+                        out=centred[:, c, cols],
+                        in0=centred[:, c, cols],
                         scalar1=gain[:, c : c + 1],
                         scalar2=bias[:, c : c + 1],
                         op0=ALU.mult,
                         op1=ALU.add,
                     )
-                for h in range(RES // HALF):
-                    cols = slice(h * HALF, (h + 1) * HALF)
-                    result = norm.tile([P, HALF, CH], F32, tag="result", bufs=3)
-                    for q in range(0, CH, QUAD):
-                        nc.scalar.copy(
-                            out=result[:, :, q : q + QUAD],
-                            in_=centred[:, q : q + QUAD, cols].rearrange("p c j -> p j c"),
-                        )
-                    nc.sync.dma_start(
-                        out=out[a * P : (a + 1) * P, cols, :].rearrange("i j c -> i (j c)"),
-                        in_=result.rearrange("p j c -> p (j c)"),
-                    )
 
-            centre_rows(0)
+            def store_half(a, h):
+                centred = planes[a]
+                cols = slice(h * HALF, (h + 1) * HALF)
+                result = late.tile([P, HALF, CH], F32, tag="result", bufs=3)
+                for q in range(0, CH, QUAD):
+                    nc.scalar.copy(
+                        out=result[:, :, q : q + QUAD],
+                        in_=centred[:, q : q + QUAD, cols].rearrange("p c j -> p j c"),
+                    )
+                nc.sync.dma_start(
+                    out=out[a * P : (a + 1) * P, cols, :].rearrange("i j c -> i (j c)"),
+                    in_=result.rearrange("p j c -> p (j c)"),
+                )
+
+            def finish_rows(a, on_vector):
+                for h in range(RES // HALF):
+                    normalise_half(a, h, on_vector)
+                    store_half(a, h)
+
+            mean_rows(2)
             quantise_tile(len(groups) - PAIRS)
-            mean_of_tile(len(groups) - 2 * PAIRS)
-            centre_rows(1)
-            variance_rows(0)
-            for a in range(TILES):
-                if a + 2 < TILES:
-                    centre_rows(a + 2)
-                if a + 3 < TILES:
-                    mean_rows(a + 3)
-                rstd_rows(a)
-                if a + 1 < TILES:
-                    variance_rows(a + 1)
-                normalise_rows(a)
+            mean_rows(3)
+            normalise_half(0, 0, 2)
+            normalise_half(0, 1, 2)
+            store_half(0, 0)
+            store_half(0, 1)
+            centre_rows(2, late)
+            variance_rows(1)
+            centre_rows(3, late)
+            rstd_rows(1)
+            normalise_half(1, 0, 2)
+            normalise_half(1, 1, 2)
+            variance_rows(2)
+            rstd_rows(2)
+            store_half(1, 0)
+            variance_rows(3)
+            rstd_rows(3)
+            store_half(1, 1)
+            finish_rows(2, 2)
+            finish_rows(3, 8)

@@ -232,12 +232,16 @@ def tile_net2_pa_kernel(
                     if g + SIG_LEAD < len(groups):
                         prepare_sigmoid(g + SIG_LEAD)
                     gate_group(g)
+                    if g == PAIRS // 2 - 1:
+                        mask_group(0)
+                        mask_group(1)
                     if g == first + 1 and a >= 0:
                         mean_rows(a)
                 if a == 1:
                     variance_rows(0)
                 for g in range(first, first + PAIRS):
-                    mask_group(g)
+                    if turn > 0 or g >= PAIRS // 2:
+                        mask_group(g)
                 if turn >= 1:
                     quantise_tile(first - PAIRS)
                 if a >= 0:
@@ -288,21 +292,21 @@ def tile_net2_pa_kernel(
             mean_rows(2)
             quantise_tile(len(groups) - PAIRS)
             mean_rows(3)
-            normalise_half(0, 0, 2)
-            normalise_half(0, 1, 2)
+            normalise_half(0, 0, 8)
+            normalise_half(0, 1, 8)
             store_half(0, 0)
             store_half(0, 1)
             centre_rows(2, late)
             variance_rows(1)
             centre_rows(3, late)
             rstd_rows(1)
-            normalise_half(1, 0, 2)
-            normalise_half(1, 1, 2)
+            normalise_half(1, 0, 8)
+            normalise_half(1, 1, 8)
             variance_rows(2)
             rstd_rows(2)
             store_half(1, 0)
             variance_rows(3)
             rstd_rows(3)
             store_half(1, 1)
-            finish_rows(2, 2)
+            finish_rows(2, 8)
             finish_rows(3, 8)

@@ -21,7 +21,7 @@ HALF = RES // 2
 QUAD = 4
 LEAD = 2
 SIG_LEAD = 3
-BANKS = 6
+BANKS = 8
 EPS = 1e-5
 
 FLOPS = 2 * RES * RES * RES * CH
@@ -51,6 +51,7 @@ def tile_net2_pa_kernel(
         nc.vector.tensor_copy(out=bias, in_=bias_bf16)
         eps = keep.tile([P, 1], F32)
         nc.vector.memset(eps, EPS)
+        warm = keep.tile([P, 1], F32)
 
         left_codes = keep.tile([P, CH, RES], U32, align_bytes=64)
         left_scales = keep.tile([P, CH, RES], U8, align_bytes=64)
@@ -71,20 +72,26 @@ def tile_net2_pa_kernel(
                 stop=stop,
             )
 
-        def mean_rows(a):
-            total = psum.tile([P, RES], F32, tag="stat")
-            for c in range(CH):
-                product_pass(total, a, c, c == 0, c == CH - 1)
-            nc.scalar.activation(out=means[:, a, :], in_=total, func=ACT.Copy, scale=1.0 / CH)
+        totals = {}
+
+        def mean_passes(a, first, last):
+            if first == 0:
+                total = psum.tile([P, RES], F32, tag="bank", bufs=BANKS)
+                totals[a] = total
+            for c in range(first, last):
+                product_pass(totals[a], a, c, c == 0, c == CH - 1)
+            if last == CH:
+                nc.scalar.activation(out=means[:, a, :], in_=totals[a], func=ACT.Copy, scale=1.0 / CH)
 
         work = ctx.enter_context(tc.tile_pool(name="work", bufs=3))
         norm = ctx.enter_context(tc.tile_pool(name="norm", bufs=2))
         planes = {}
         squares = {}
+        variances = {}
         rstds_t = {}
         rstds = {}
 
-        def centre_rows(a, pool):
+        def centre_rows(a, pool, between=None):
             centred = pool.tile([P, CH, RES], F32, tag="centred", bufs=2)
             squared = norm.tile([P, CH, RES], F32, tag="squared", bufs=2)
             for c in range(CH):
@@ -95,30 +102,42 @@ def tile_net2_pa_kernel(
                     nc.scalar.activation(
                         out=squared[:, c - 1 : c + 1, :], in_=centred[:, c - 1 : c + 1, :], func=ACT.Square
                     )
+                    if between is not None:
+                        between(c // 2)
             planes[a] = centred
             squares[a] = squared
 
-        def variance_rows(a):
-            var_t = psum.tile([P, TILES, P], F32, tag="stat")
-            for b in range(TILES):
-                for c in range(CH):
-                    nc.tensor.matmul(
-                        out=var_t[:, b, :],
-                        lhsT=squares[a][:, c, b * P : (b + 1) * P],
-                        rhs=ident_f32,
-                        is_transpose=True,
-                        start=(c == 0),
-                        stop=(c == CH - 1),
-                    )
+        def variance_block(a, b):
+            if b == 0:
+                var_t = psum.tile([P, TILES, P], F32, tag="bank", bufs=BANKS)
+                variances[a] = var_t
+            for c in range(CH):
+                nc.tensor.matmul(
+                    out=variances[a][:, b, :],
+                    lhsT=squares[a][:, c, b * P : (b + 1) * P],
+                    rhs=ident_f32,
+                    is_transpose=True,
+                    start=(c == 0),
+                    stop=(c == CH - 1),
+                )
+
+        def variance_step(a, n):
+            if n < 2:
+                variance_block(a, 2 * n)
+                variance_block(a, 2 * n + 1)
+            elif n == 2:
+                deviation_rows(a)
+
+        def deviation_rows(a):
             rstd_t = norm.tile([P, TILES, P], F32, tag="rstd_t")
             nc.scalar.activation(
-                out=rstd_t, in_=var_t, func=ACT.Abs_reciprocal_sqrt, scale=1.0 / CH, bias=eps
+                out=rstd_t, in_=variances[a], func=ACT.Abs_reciprocal_sqrt, scale=1.0 / CH, bias=eps
             )
             rstds_t[a] = rstd_t
 
         def rstd_rows(a):
-            if a == 0:
-                rstd = psum.tile([P, TILES, P], F32, tag="rstd")
+            if a % 2 == 0:
+                rstd = psum.tile([P, TILES, P], F32, tag="bank", bufs=BANKS)
             else:
                 rstd = psum.tile([P, TILES, P], F32, tag="bank", bufs=BANKS)
             for b in range(TILES):
@@ -161,7 +180,7 @@ def tile_net2_pa_kernel(
                 sigmoids[g] = sig
 
             def transpose_mask(n):
-                mask_t = psum.tile([P, PACK, P], BF16, tag="stat")
+                mask_t = psum.tile([P, PACK, P], BF16, tag="bank", bufs=BANKS)
                 for t in range(PACK):
                     nc.tensor.transpose(mask_t[:, t, :], mask_rows[:, n, t : RES : PACK], ident_bf16)
                 nc.scalar.copy(out=mask_kt[:, n], in_=mask_t.rearrange("p t r -> p r t"))
@@ -226,37 +245,41 @@ def tile_net2_pa_kernel(
             for turn in range(2 * TILES):
                 first = turn * PAIRS
                 a = turn - TILES - 2
-                for g in range(first, first + PAIRS):
+                for w in range(PAIRS):
+                    g = first + w
                     if g + LEAD < len(groups):
                         prepare_projection(g + LEAD)
                     if g + SIG_LEAD < len(groups):
                         prepare_sigmoid(g + SIG_LEAD)
+                    if a >= 0:
+                        mean_passes(a, 2 * w, 2 * w + 2)
                     gate_group(g)
                     if g == PAIRS // 2 - 1:
                         mask_group(0)
                         mask_group(1)
-                    if g == first + 1 and a >= 0:
-                        mean_rows(a)
-                if a == 1:
-                    variance_rows(0)
                 for g in range(first, first + PAIRS):
                     if turn > 0 or g >= PAIRS // 2:
                         mask_group(g)
                 if turn >= 1:
                     quantise_tile(first - PAIRS)
-                if a >= 0:
-                    centre_rows(a, norm)
+                if a == 0:
+                    centre_rows(0, norm)
+                if a == 1:
+                    nc.scalar.activation(out=warm, in_=eps, func=ACT.Abs_reciprocal_sqrt)
+                    centre_rows(1, norm, lambda n: variance_step(0, n))
+            mean_passes(2, 0, 8)
+            quantise_tile(len(groups) - PAIRS)
             rstd_rows(0)
 
         with tc.tile_pool(name="late", bufs=2) as late:
 
-            def normalise_half(a, h, on_vector):
+            def normalise(a, start, width, on_vector):
                 centred = planes[a]
-                cols = slice(h * HALF, (h + 1) * HALF)
+                cols = slice(start, start + width)
                 nc.vector.tensor_tensor(
                     out=centred[:, :, cols],
                     in0=centred[:, :, cols],
-                    in1=rstds[a][:, cols].unsqueeze(1).to_broadcast([P, CH, HALF]),
+                    in1=rstds[a][:, cols].unsqueeze(1).to_broadcast([P, CH, width]),
                     op=ALU.mult,
                 )
                 for c in range(CH):
@@ -270,43 +293,45 @@ def tile_net2_pa_kernel(
                         op1=ALU.add,
                     )
 
-            def store_half(a, h):
+            def store(a, start, width, on_vector=0):
                 centred = planes[a]
-                cols = slice(h * HALF, (h + 1) * HALF)
-                result = late.tile([P, HALF, CH], F32, tag="result", bufs=3)
-                for q in range(0, CH, QUAD):
-                    nc.scalar.copy(
-                        out=result[:, :, q : q + QUAD],
+                cols = slice(start, start + width)
+                result = late.tile([P, HALF, CH], F32, tag="result", bufs=4)
+                for n, q in enumerate(range(0, CH, QUAD)):
+                    copy = nc.vector.tensor_copy if n < on_vector else nc.scalar.copy
+                    copy(
+                        out=result[:, :width, q : q + QUAD],
                         in_=centred[:, q : q + QUAD, cols].rearrange("p c j -> p j c"),
                     )
                 nc.sync.dma_start(
                     out=out[a * P : (a + 1) * P, cols, :].rearrange("i j c -> i (j c)"),
-                    in_=result.rearrange("p j c -> p (j c)"),
+                    in_=result[:, :width].rearrange("p j c -> p (j c)"),
                 )
 
-            def finish_rows(a, on_vector):
-                for h in range(RES // HALF):
-                    normalise_half(a, h, on_vector)
-                    store_half(a, h)
-
-            mean_rows(2)
-            quantise_tile(len(groups) - PAIRS)
-            mean_rows(3)
-            normalise_half(0, 0, 8)
-            normalise_half(0, 1, 8)
-            store_half(0, 0)
-            store_half(0, 1)
-            centre_rows(2, late)
-            variance_rows(1)
-            centre_rows(3, late)
+            normalise(0, 0, HALF, 0)
+            centre_rows(2, late, lambda n: variance_step(1, n))
+            store(0, 0, HALF)
+            mean_passes(3, 0, 8)
             rstd_rows(1)
-            normalise_half(1, 0, 8)
-            normalise_half(1, 1, 8)
-            variance_rows(2)
+            normalise(0, HALF, HALF, 0)
+            normalise(1, 0, HALF, 0)
+            store(0, HALF, HALF)
+            centre_rows(3, late, lambda n: variance_step(2, n))
+            store(1, 0, HALF)
             rstd_rows(2)
-            store_half(1, 0)
-            variance_rows(3)
+            normalise(1, HALF, HALF, 0)
+            for b in range(TILES):
+                variance_block(3, b)
+            deviation_rows(3)
             rstd_rows(3)
-            store_half(1, 1)
-            finish_rows(2, 8)
-            finish_rows(3, 8)
+            normalise(2, 0, HALF, 0)
+            store(1, HALF, HALF)
+            normalise(2, HALF, HALF, 0)
+            store(2, 0, HALF)
+            normalise(3, 0, HALF, 6)
+            store(2, HALF, HALF, 1)
+            store(3, 0, HALF, 1)
+            normalise(3, HALF, HALF // 2, 6)
+            store(3, HALF, HALF // 2, 1)
+            normalise(3, HALF + HALF // 2, HALF // 2, 6)
+            store(3, HALF + HALF // 2, HALF // 2, 1)

@@ -234,13 +234,11 @@ def tile_net2_pa_kernel(
 
             load_rows(0)
             nc.sync.dma_start(out=mask_rows, in_=mask.rearrange("(n r) k -> r n k", r=P))
-            for g in range(LEAD):
+            for g in range(SIG_LEAD):
                 sigmoid_group(g)
             for g in range(LEAD):
                 transposed[g] = transposed_pair(0, g)
             transpose_mask(0)
-            for g in range(LEAD, SIG_LEAD):
-                sigmoid_group(g)
 
             for turn in range(2 * TILES):
                 first = turn * PAIRS
@@ -251,8 +249,8 @@ def tile_net2_pa_kernel(
                         prepare_projection(g + LEAD)
                     if g + SIG_LEAD < len(groups):
                         prepare_sigmoid(g + SIG_LEAD)
-                    if a >= 0:
-                        mean_passes(a, 2 * w, 2 * w + 2)
+                    if a >= 0 and w < 2:
+                        mean_passes(a, 4 * w, 4 * w + 4)
                     gate_group(g)
                     if g == PAIRS // 2 - 1:
                         mask_group(0)
@@ -310,28 +308,28 @@ def tile_net2_pa_kernel(
 
             normalise(0, 0, HALF, 0)
             centre_rows(2, late, lambda n: variance_step(1, n))
-            store(0, 0, HALF)
             mean_passes(3, 0, 8)
             rstd_rows(1)
             normalise(0, HALF, HALF, 0)
+            store(0, 0, HALF, 0)
             normalise(1, 0, HALF, 0)
-            store(0, HALF, HALF)
             centre_rows(3, late, lambda n: variance_step(2, n))
-            store(1, 0, HALF)
+            store(0, HALF, HALF, 0)
             rstd_rows(2)
             normalise(1, HALF, HALF, 0)
             for b in range(TILES):
                 variance_block(3, b)
+            store(1, 0, HALF, 1)
             deviation_rows(3)
             rstd_rows(3)
             normalise(2, 0, HALF, 0)
-            store(1, HALF, HALF)
+            store(1, HALF, HALF, 1)
             normalise(2, HALF, HALF, 0)
-            store(2, 0, HALF)
-            normalise(3, 0, HALF, 6)
+            store(2, 0, HALF, 1)
+            normalise(3, 0, HALF, 8)
             store(2, HALF, HALF, 1)
             store(3, 0, HALF, 1)
-            normalise(3, HALF, HALF // 2, 6)
+            normalise(3, HALF, HALF // 2, 8)
             store(3, HALF, HALF // 2, 1)
-            normalise(3, HALF + HALF // 2, HALF // 2, 6)
+            normalise(3, HALF + HALF // 2, HALF // 2, 8)
             store(3, HALF + HALF // 2, HALF // 2, 1)

@@ -271,7 +271,7 @@ def tile_net2_pa_kernel(
 
         with tc.tile_pool(name="late", bufs=2) as late:
 
-            def normalise(a, start, width, on_vector):
+            def normalise(a, start, width):
                 centred = planes[a]
                 cols = slice(start, start + width)
                 nc.vector.tensor_tensor(
@@ -280,7 +280,20 @@ def tile_net2_pa_kernel(
                     in1=rstds[a][:, cols].unsqueeze(1).to_broadcast([P, CH, width]),
                     op=ALU.mult,
                 )
+
+            def scale_shift(a, start, width, on_vector=0, on_scalar=0):
+                centred = planes[a]
+                cols = slice(start, start + width)
                 for c in range(CH):
+                    if c >= CH - on_scalar:
+                        nc.scalar.activation(
+                            out=centred[:, c, cols],
+                            in_=centred[:, c, cols],
+                            func=ACT.Identity,
+                            scale=gain[:, c : c + 1],
+                            bias=bias[:, c : c + 1],
+                        )
+                        continue
                     engine = nc.vector if c < on_vector else nc.gpsimd
                     engine.tensor_scalar(
                         out=centred[:, c, cols],
@@ -306,30 +319,39 @@ def tile_net2_pa_kernel(
                     in_=result[:, :width].rearrange("p j c -> p (j c)"),
                 )
 
-            normalise(0, 0, HALF, 0)
+            normalise(0, 0, HALF)
+            scale_shift(0, 0, HALF, 0, 0)
             centre_rows(2, late, lambda n: variance_step(1, n))
             mean_passes(3, 0, 8)
             rstd_rows(1)
-            normalise(0, HALF, HALF, 0)
+            normalise(0, HALF, HALF)
+            scale_shift(0, HALF, HALF, 0, 0)
             store(0, 0, HALF, 0)
-            normalise(1, 0, HALF, 0)
+            normalise(1, 0, HALF)
+            scale_shift(1, 0, HALF, 0, 0)
             centre_rows(3, late, lambda n: variance_step(2, n))
             store(0, HALF, HALF, 0)
             rstd_rows(2)
-            normalise(1, HALF, HALF, 0)
+            normalise(1, HALF, HALF)
+            scale_shift(1, HALF, HALF, 0, 0)
             for b in range(TILES):
                 variance_block(3, b)
-            store(1, 0, HALF, 1)
+            store(1, 0, HALF, 0)
             deviation_rows(3)
             rstd_rows(3)
-            normalise(2, 0, HALF, 0)
-            store(1, HALF, HALF, 1)
-            normalise(2, HALF, HALF, 0)
-            store(2, 0, HALF, 1)
-            normalise(3, 0, HALF, 8)
-            store(2, HALF, HALF, 1)
+            normalise(2, 0, HALF)
+            scale_shift(2, 0, HALF, 0, 0)
+            store(1, HALF, HALF, 0)
+            normalise(2, HALF, HALF)
+            scale_shift(2, HALF, HALF, 0, 0)
+            store(2, 0, HALF, 0)
+            normalise(3, 0, HALF)
+            scale_shift(3, 0, HALF, 8)
+            store(2, HALF, HALF, 0)
             store(3, 0, HALF, 1)
-            normalise(3, HALF, HALF // 2, 8)
+            normalise(3, HALF, HALF // 2)
+            scale_shift(3, HALF, HALF // 2, 8)
             store(3, HALF, HALF // 2, 1)
-            normalise(3, HALF + HALF // 2, HALF // 2, 8)
+            normalise(3, HALF + HALF // 2, HALF // 2)
+            scale_shift(3, HALF + HALF // 2, HALF // 2, 8)
             store(3, HALF + HALF // 2, HALF // 2, 1)

@@ -320,34 +320,34 @@ def tile_net2_pa_kernel(
                 )
 
             normalise(0, 0, HALF)
-            scale_shift(0, 0, HALF, 0, 0)
+            scale_shift(0, 0, HALF, 0)
             centre_rows(2, late, lambda n: variance_step(1, n))
             mean_passes(3, 0, 8)
             rstd_rows(1)
             normalise(0, HALF, HALF)
-            scale_shift(0, HALF, HALF, 0, 0)
+            scale_shift(0, HALF, HALF, 0)
             store(0, 0, HALF, 0)
             normalise(1, 0, HALF)
-            scale_shift(1, 0, HALF, 0, 0)
+            scale_shift(1, 0, HALF, 0)
             centre_rows(3, late, lambda n: variance_step(2, n))
             store(0, HALF, HALF, 0)
             rstd_rows(2)
             normalise(1, HALF, HALF)
-            scale_shift(1, HALF, HALF, 0, 0)
+            scale_shift(1, HALF, HALF, 0)
             for b in range(TILES):
                 variance_block(3, b)
             store(1, 0, HALF, 0)
             deviation_rows(3)
             rstd_rows(3)
             normalise(2, 0, HALF)
-            scale_shift(2, 0, HALF, 0, 0)
+            scale_shift(2, 0, HALF, 8)
             store(1, HALF, HALF, 0)
             normalise(2, HALF, HALF)
-            scale_shift(2, HALF, HALF, 0, 0)
+            scale_shift(2, HALF, HALF, 8)
             store(2, 0, HALF, 0)
             normalise(3, 0, HALF)
             scale_shift(3, 0, HALF, 8)
-            store(2, HALF, HALF, 0)
+            store(2, HALF, HALF, 1)
             store(3, 0, HALF, 1)
             normalise(3, HALF, HALF // 2)
             scale_shift(3, HALF, HALF // 2, 8)

@@ -42,13 +42,9 @@ def tile_net2_pa_kernel(
         make_identity(nc, ident_bf16)
 
         gain_bf16 = keep.tile([P, CH], BF16)
-        nc.scalar.dma_start(out=gain_bf16, in_=ln_c_g.partition_broadcast(P))
         bias_bf16 = keep.tile([P, CH], BF16)
-        nc.scalar.dma_start(out=bias_bf16, in_=ln_c_b.partition_broadcast(P))
         gain = keep.tile([P, CH], F32)
-        nc.vector.tensor_copy(out=gain, in_=gain_bf16)
         bias = keep.tile([P, CH], F32)
-        nc.vector.tensor_copy(out=bias, in_=bias_bf16)
         eps = keep.tile([P, 1], F32)
         nc.vector.memset(eps, EPS)
         warm = keep.tile([P, 1], F32)
@@ -241,6 +237,12 @@ def tile_net2_pa_kernel(
             transpose_mask(0)
 
             for turn in range(2 * TILES):
+                if turn == 2:
+                    nc.sync.dma_start(out=gain_bf16, in_=ln_c_g.partition_broadcast(P))
+                    nc.sync.dma_start(out=bias_bf16, in_=ln_c_b.partition_broadcast(P))
+                if turn == TILES:
+                    nc.vector.tensor_copy(out=gain, in_=gain_bf16)
+                    nc.vector.tensor_copy(out=bias, in_=bias_bf16)
                 first = turn * PAIRS
                 a = turn - TILES - 2
                 for w in range(PAIRS):

@@ -103,42 +103,39 @@ def tile_net2_pa_kernel(
             planes[a] = centred
             squares[a] = squared
 
-        def variance_block(a, b):
-            if b == 0:
-                var_t = psum.tile([P, TILES, P], F32, tag="bank", bufs=BANKS)
-                variances[a] = var_t
-            for c in range(CH):
-                nc.tensor.matmul(
-                    out=variances[a][:, b, :],
-                    lhsT=squares[a][:, c, b * P : (b + 1) * P],
-                    rhs=ident_f32,
-                    is_transpose=True,
-                    start=(c == 0),
-                    stop=(c == CH - 1),
-                )
+        def variance_half(a, h):
+            var_t = psum.tile([P, TILES // 2, P], F32, tag="bank", bufs=BANKS)
+            for b in range(TILES // 2):
+                j0 = h * HALF + b * P
+                for c in range(CH):
+                    nc.tensor.matmul(
+                        out=var_t[:, b, :],
+                        lhsT=squares[a][:, c, j0 : j0 + P],
+                        rhs=ident_f32,
+                        is_transpose=True,
+                        start=(c == 0),
+                        stop=(c == CH - 1),
+                    )
+            variances[(a, h)] = var_t
 
         def variance_step(a, n):
             if n < 2:
-                variance_block(a, 2 * n)
-                variance_block(a, 2 * n + 1)
-            elif n == 2:
-                deviation_rows(a)
+                variance_half(a, n)
+            if 0 < n < 3:
+                deviation_half(a, n - 1)
 
-        def deviation_rows(a):
-            rstd_t = norm.tile([P, TILES, P], F32, tag="rstd_t")
+        def deviation_half(a, h):
+            rstd_t = norm.tile([P, TILES // 2, P], F32, tag="rstd_t", bufs=4)
             nc.scalar.activation(
-                out=rstd_t, in_=variances[a], func=ACT.Abs_reciprocal_sqrt, scale=1.0 / CH, bias=eps
+                out=rstd_t, in_=variances[(a, h)], func=ACT.Abs_reciprocal_sqrt, scale=1.0 / CH, bias=eps
             )
-            rstds_t[a] = rstd_t
+            rstds_t[(a, h)] = rstd_t
 
-        def rstd_rows(a):
-            if a % 2 == 0:
-                rstd = psum.tile([P, TILES, P], F32, tag="bank", bufs=BANKS)
-            else:
-                rstd = psum.tile([P, TILES, P], F32, tag="bank", bufs=BANKS)
-            for b in range(TILES):
-                nc.tensor.transpose(rstd[:, b, :], rstds_t[a][:, b, :], ident_f32)
-            rstds[a] = rstd.rearrange("p b j -> p (b j)")
+        def rstd_half(a, h):
+            rstd = psum.tile([P, TILES // 2, P], F32, tag="bank", bufs=BANKS)
+            for b in range(TILES // 2):
+                nc.tensor.transpose(rstd[:, b, :], rstds_t[(a, h)][:, b, :], ident_f32)
+            rstds[(a, h)] = rstd.rearrange("p b j -> p (b j)")
 
         with tc.tile_pool(name="loads", bufs=3) as loads:
             sides = (
@@ -269,7 +266,8 @@ def tile_net2_pa_kernel(
                     centre_rows(1, norm, lambda n: variance_step(0, n))
             mean_passes(2, 0, 8)
             quantise_tile(len(groups) - PAIRS)
-            rstd_rows(0)
+            for h in range(2):
+                rstd_half(0, h)
 
         with tc.tile_pool(name="late", bufs=2) as late:
 
@@ -279,7 +277,7 @@ def tile_net2_pa_kernel(
                 nc.vector.tensor_tensor(
                     out=centred[:, :, cols],
                     in0=centred[:, :, cols],
-                    in1=rstds[a][:, cols].unsqueeze(1).to_broadcast([P, CH, width]),
+                    in1=rstds[(a, start // HALF)][:, start % HALF : start % HALF + width].unsqueeze(1).to_broadcast([P, CH, width]),
                     op=ALU.mult,
                 )
 
@@ -322,30 +320,34 @@ def tile_net2_pa_kernel(
                 )
 
             normalise(0, 0, HALF)
-            scale_shift(0, 0, HALF, 0)
+            scale_shift(0, 0, HALF)
             centre_rows(2, late, lambda n: variance_step(1, n))
             mean_passes(3, 0, 8)
-            rstd_rows(1)
+            rstd_half(1, 0)
+            rstd_half(1, 1)
             normalise(0, HALF, HALF)
-            scale_shift(0, HALF, HALF, 0)
+            scale_shift(0, HALF, HALF)
             store(0, 0, HALF, 0)
             normalise(1, 0, HALF)
-            scale_shift(1, 0, HALF, 0)
+            scale_shift(1, 0, HALF)
             centre_rows(3, late, lambda n: variance_step(2, n))
             store(0, HALF, HALF, 0)
-            rstd_rows(2)
+            rstd_half(2, 0)
+            rstd_half(2, 1)
             normalise(1, HALF, HALF)
-            scale_shift(1, HALF, HALF, 0)
-            for b in range(TILES):
-                variance_block(3, b)
+            scale_shift(1, HALF, HALF)
+            variance_half(3, 0)
+            variance_half(3, 1)
             store(1, 0, HALF, 0)
-            deviation_rows(3)
-            rstd_rows(3)
+            deviation_half(3, 0)
+            rstd_half(3, 0)
             normalise(2, 0, HALF)
-            scale_shift(2, 0, HALF, 8)
-            store(1, HALF, HALF, 0)
+            deviation_half(3, 1)
+            rstd_half(3, 1)
             normalise(2, HALF, HALF)
+            scale_shift(2, 0, HALF, 8)
             scale_shift(2, HALF, HALF, 8)
+            store(1, HALF, HALF, 1)
             store(2, 0, HALF, 0)
             normalise(3, 0, HALF)
             scale_shift(3, 0, HALF, 8)

@@ -49,19 +49,18 @@ def tile_net2_pa_kernel(
         nc.vector.memset(eps, EPS)
         warm = keep.tile([P, 1], F32)
 
-        left_codes = keep.tile([P, CH, RES], U32, align_bytes=64)
-        left_scales = keep.tile([P, CH, RES], U8, align_bytes=64)
+        left_codes = keep.tile([P, TILES, CH, P], U32, align_bytes=64)
+        left_scales = keep.tile([P, TILES, CH, P], U8, align_bytes=64)
         right_codes = keep.tile([P, CH, RES], U32, align_bytes=64)
         right_scales = keep.tile([P, CH, RES], U8, align_bytes=64)
         mask_kt = keep.tile([P, TILES, P, PACK], BF16)
         means = keep.tile([P, TILES, RES], F32)
 
         def product_pass(acc, a, c, start, stop):
-            rows = slice(a * P, (a + 1) * P)
             nc.tensor.matmul_mx(
                 out=acc,
-                lhsT=left_codes[:, c, rows].bitcast(FP8X4),
-                lhsT_scale=left_scales[:, c, rows],
+                lhsT=left_codes[:, a, c].bitcast(FP8X4),
+                lhsT_scale=left_scales[:, a, c],
                 rhs=right_codes[:, c, :].bitcast(FP8X4),
                 rhs_scale=right_scales[:, c, :],
                 start=start,
@@ -139,8 +138,8 @@ def tile_net2_pa_kernel(
 
         with tc.tile_pool(name="loads", bufs=3) as loads:
             sides = (
-                (right_proj, right_gate, right_codes, right_scales),
-                (left_proj, left_gate, left_codes, left_scales),
+                (right_proj, right_gate),
+                (left_proj, left_gate),
             )
             groups = [(s, n, w) for s in range(2) for n in range(TILES) for w in range(PAIRS)]
             mask_rows = loads.tile([P, TILES, RES], BF16, bufs=1)
@@ -158,6 +157,8 @@ def tile_net2_pa_kernel(
                         out=rows, in_=sides[s][which][n * P : (n + 1) * P].rearrange("r k c -> r (k c)")
                     )
                     loaded[(which, s, n)] = rows
+                if s == 0:
+                    nc.sync.dma_start(out=mask_rows[:, n], in_=mask[n * P : (n + 1) * P])
 
             def transposed_pair(which, g):
                 s, n, w = groups[g]
@@ -197,7 +198,10 @@ def tile_net2_pa_kernel(
 
             def mask_group(g):
                 s, n, w = groups[g]
-                if w < PAIRS // 2:
+                if w == 1 and (s, n) == (1, 2):
+                    engine = nc.gpsimd
+                    kept = work.tile([P, 2, P, PACK], BF16, tag="kept_extra", bufs=1, align_bytes=64)
+                elif w < PAIRS // 2:
                     engine = nc.vector
                     kept = work.tile([P, 2, P, PACK], BF16, tag="kept_vector", bufs=PAIRS, align_bytes=64)
                 else:
@@ -213,12 +217,21 @@ def tile_net2_pa_kernel(
 
             def quantise_group(g):
                 s, n, w = groups[g]
+                kept = masked[g].rearrange("p e r t -> p (e r t)")
+                if s == 1:
+                    pair = slice(2 * w, 2 * w + 2)
+                    nc.vector.quantize_mx(
+                        out=left_codes[:, n, pair].rearrange("p c r -> p (c r)").bitcast(FP8X4),
+                        scales=left_scales[:, n, pair].rearrange("p c r -> p (c r)"),
+                        in_=kept,
+                    )
+                    return
                 rows = slice(n * P, (n + 1) * P)
                 for e in range(2):
                     nc.vector.quantize_mx(
-                        out=sides[s][2][:, 2 * w + e, rows].bitcast(FP8X4),
-                        scales=sides[s][3][:, 2 * w + e, rows],
-                        in_=masked[g][:, e].rearrange("p r t -> p (r t)"),
+                        out=right_codes[:, 2 * w + e, rows].bitcast(FP8X4),
+                        scales=right_scales[:, 2 * w + e, rows],
+                        in_=kept[:, e * RES : (e + 1) * RES],
                     )
 
             def quantise_tile(first):
@@ -226,7 +239,6 @@ def tile_net2_pa_kernel(
                     quantise_group(g)
 
             load_rows(0)
-            nc.sync.dma_start(out=mask_rows, in_=mask.rearrange("(n r) k -> r n k", r=P))
             for g in range(SIG_LEAD):
                 sigmoid_group(g)
             for g in range(LEAD):
@@ -248,13 +260,13 @@ def tile_net2_pa_kernel(
                         prepare_projection(g + LEAD)
                     if g + SIG_LEAD < len(groups):
                         prepare_sigmoid(g + SIG_LEAD)
-                    if a >= 0 and w < 2:
-                        mean_passes(a, 4 * w, 4 * w + 4)
+                    if a >= 0 and 0 < w < 3:
+                        mean_passes(a, 4 * w - 4, 4 * w)
                     gate_group(g)
                     if g == PAIRS // 2 - 1:
                         mask_group(0)
                         mask_group(1)
-                for g in range(first, first + PAIRS):
+                for g in (first, first + 2, first + 3, first + 1) if turn == 6 else range(first, first + PAIRS):
                     if turn > 0 or g >= PAIRS // 2:
                         mask_group(g)
                 if turn >= 1:
@@ -320,22 +332,22 @@ def tile_net2_pa_kernel(
                 )
 
             normalise(0, 0, HALF)
-            scale_shift(0, 0, HALF)
+            scale_shift(0, 0, HALF, 0)
             centre_rows(2, late, lambda n: variance_step(1, n))
             mean_passes(3, 0, 8)
             rstd_half(1, 0)
             rstd_half(1, 1)
             normalise(0, HALF, HALF)
-            scale_shift(0, HALF, HALF)
+            scale_shift(0, HALF, HALF, 0)
             store(0, 0, HALF, 0)
             normalise(1, 0, HALF)
-            scale_shift(1, 0, HALF)
+            scale_shift(1, 0, HALF, 0)
             centre_rows(3, late, lambda n: variance_step(2, n))
             store(0, HALF, HALF, 0)
             rstd_half(2, 0)
             rstd_half(2, 1)
             normalise(1, HALF, HALF)
-            scale_shift(1, HALF, HALF)
+            scale_shift(1, HALF, HALF, 0)
             variance_half(3, 0)
             variance_half(3, 1)
             store(1, 0, HALF, 0)

from contextlib import ExitStack

import concourse.mybir as mybir
from concourse.masks import make_identity

BF16 = mybir.dt.bfloat16
F32 = mybir.dt.float32
U32 = mybir.dt.uint32
U8 = mybir.dt.uint8
FP8X4 = mybir.dt.float8_e4m3fn_x4
ACT = mybir.ActivationFunctionType
ALU = mybir.AluOpType

P = 128
PACK = 4
RES = 512
CH = 8
PAIRS = CH // 2
TILES = RES // P
HALF = RES // 2
QUAD = 4
LEAD = 2
SIG_LEAD = 3
BANKS = 8
EPS = 1e-5

FLOPS = 2 * RES * RES * RES * CH


def tile_net2_pa_kernel(
    tc, left_proj, left_gate, right_proj, right_gate, mask, ln_c_g, ln_c_b, out
):
    nc = tc.nc
    with ExitStack() as ctx:
        ctx.enter_context(tc.manual_schedule())
        keep = ctx.enter_context(tc.tile_pool(name="keep", bufs=1))
        psum = ctx.enter_context(tc.psum_pool(name="psum", bufs=1))

        ident_f32 = keep.tile([P, P], F32)
        make_identity(nc, ident_f32)
        ident_bf16 = keep.tile([P, P], BF16)
        make_identity(nc, ident_bf16)

        gain_bf16 = keep.tile([P, CH], BF16)
        bias_bf16 = keep.tile([P, CH], BF16)
        gain = keep.tile([P, CH], F32)
        bias = keep.tile([P, CH], F32)
        eps = keep.tile([P, 1], F32)
        nc.vector.memset(eps, EPS)
        warm = keep.tile([P, 1], F32)

        left_codes = keep.tile([P, TILES, CH, P], U32, align_bytes=64)
        left_scales = keep.tile([P, TILES, CH, P], U8, align_bytes=64)
        right_codes = keep.tile([P, CH, RES], U32, align_bytes=64)
        right_scales = keep.tile([P, CH, RES], U8, align_bytes=64)
        mask_kt = keep.tile([P, TILES, P, PACK], BF16)
        means = keep.tile([P, TILES, RES], F32)

        def product_pass(acc, a, c, start, stop):
            nc.tensor.matmul_mx(
                out=acc,
                lhsT=left_codes[:, a, c].bitcast(FP8X4),
                lhsT_scale=left_scales[:, a, c],
                rhs=right_codes[:, c, :].bitcast(FP8X4),
                rhs_scale=right_scales[:, c, :],
                start=start,
                stop=stop,
            )

        totals = {}

        def mean_passes(a, first, last):
            if first == 0:
                total = psum.tile([P, RES], F32, tag="bank", bufs=BANKS)
                totals[a] = total
            for c in range(first, last):
                product_pass(totals[a], a, c, c == 0, c == CH - 1)
            if last == CH:
                nc.scalar.activation(out=means[:, a, :], in_=totals[a], func=ACT.Copy, scale=1.0 / CH)

        work = ctx.enter_context(tc.tile_pool(name="work", bufs=3))
        norm = ctx.enter_context(tc.tile_pool(name="norm", bufs=2))
        planes = {}
        squares = {}
        variances = {}
        rstds_t = {}
        rstds = {}

        def centre_rows(a, pool, between=None):
            centred = pool.tile([P, CH, RES], F32, tag="centred", bufs=2)
            squared = norm.tile([P, CH, RES], F32, tag="squared", bufs=2)
            for c in range(CH):
                x = psum.tile([P, RES], F32, tag="bank", bufs=BANKS)
                product_pass(x, a, c, True, True)
                nc.vector.tensor_tensor(out=centred[:, c, :], in0=x, in1=means[:, a, :], op=ALU.subtract)
                if c % 2 == 1:
                    nc.scalar.activation(
                        out=squared[:, c - 1 : c + 1, :], in_=centred[:, c - 1 : c + 1, :], func=ACT.Square
                    )
                    if between is not None:
                        between(c // 2)
            planes[a] = centred
            squares[a] = squared

        def variance_half(a, h):
            var_t = psum.tile([P, TILES // 2, P], F32, tag="bank", bufs=BANKS)
            for b in range(TILES // 2):
                j0 = h * HALF + b * P
                for c in range(CH):
                    nc.tensor.matmul(
                        out=var_t[:, b, :],
                        lhsT=squares[a][:, c, j0 : j0 + P],
                        rhs=ident_f32,
                        is_transpose=True,
                        start=(c == 0),
                        stop=(c == CH - 1),
                    )
            variances[(a, h)] = var_t

        def variance_step(a, n):
            if n < 2:
                variance_half(a, n)
            if 0 < n < 3:
                deviation_half(a, n - 1)

        def deviation_half(a, h):
            rstd_t = norm.tile([P, TILES // 2, P], F32, tag="rstd_t", bufs=4)
            nc.scalar.activation(
                out=rstd_t, in_=variances[(a, h)], func=ACT.Abs_reciprocal_sqrt, scale=1.0 / CH, bias=eps
            )
            rstds_t[(a, h)] = rstd_t

        def rstd_half(a, h):
            rstd = psum.tile([P, TILES // 2, P], F32, tag="bank", bufs=BANKS)
            for b in range(TILES // 2):
                nc.tensor.transpose(rstd[:, b, :], rstds_t[(a, h)][:, b, :], ident_f32)
            rstds[(a, h)] = rstd.rearrange("p b j -> p (b j)")

        with tc.tile_pool(name="loads", bufs=3) as loads:
            sides = (
                (right_proj, right_gate),
                (left_proj, left_gate),
            )
            groups = [(s, n, w) for s in range(2) for n in range(TILES) for w in range(PAIRS)]
            mask_rows = loads.tile([P, TILES, RES], BF16, bufs=1)
            loaded = {}
            sigmoids = {}
            transposed = {}
            gated = {}
            masked = {}

            def load_rows(g):
                s, n, w = groups[g]
                for which in (1, 0):
                    rows = loads.tile([P, RES * CH], BF16, tag="rows%d" % which)
                    nc.sync.dma_start(
                        out=rows, in_=sides[s][which][n * P : (n + 1) * P].rearrange("r k c -> r (k c)")
                    )
                    loaded[(which, s, n)] = rows
                if s == 0:
                    nc.sync.dma_start(out=mask_rows[:, n], in_=mask[n * P : (n + 1) * P])

            def transposed_pair(which, g):
                s, n, w = groups[g]
                words = loaded[(which, s, n)].bitcast(F32).rearrange("r (k w) -> r k w", w=PAIRS)
                bank = psum.tile([P, PACK, P], F32, tag="bank", bufs=BANKS)
                for t in range(PACK):
                    nc.tensor.transpose(bank[:, t, :], words[:, t : RES : PACK, w], ident_f32)
                return bank.bitcast(BF16).rearrange("p t (r e) -> p e r t", e=2)

            def sigmoid_group(g):
                sig = work.tile([P, 2, P, PACK], F32, tag="sig", bufs=SIG_LEAD + 2)
                nc.scalar.activation(out=sig, in_=transposed_pair(1, g), func=ACT.Sigmoid)
                sigmoids[g] = sig

            def transpose_mask(n):
                mask_t = psum.tile([P, PACK, P], BF16, tag="bank", bufs=BANKS)
                for t in range(PACK):
                    nc.tensor.transpose(mask_t[:, t, :], mask_rows[:, n, t : RES : PACK], ident_bf16)
                nc.scalar.copy(out=mask_kt[:, n], in_=mask_t.rearrange("p t r -> p r t"))

            def prepare_sigmoid(g):
                s, n, w = groups[g]
                if w == 0:
                    load_rows(g)
                sigmoid_group(g)

            def prepare_projection(g):
                s, n, w = groups[g]
                transposed[g] = transposed_pair(0, g)
                if s == 0 and w == 0:
                    transpose_mask(n)

            def gate_group(g):
                product = work.tile([P, 2, P, PACK], BF16, tag="product", bufs=6)
                nc.vector.tensor_tensor(out=product, in0=transposed[g], in1=sigmoids[g], op=ALU.mult)
                gated[g] = product

            def mask_group(g):
                s, n, w = groups[g]
                if w == 1 and (s, n) == (1, 2):
                    engine = nc.gpsimd
                    kept = work.tile([P, 2, P, PACK], BF16, tag="kept_extra", bufs=1, align_bytes=64)
                elif w < PAIRS // 2:
                    engine = nc.vector
                    kept = work.tile([P, 2, P, PACK], BF16, tag="kept_vector", bufs=PAIRS, align_bytes=64)
                else:
                    engine = nc.gpsimd
                    kept = work.tile([P, 2, P, PACK], BF16, tag="kept_gpsimd", bufs=PAIRS // 2, align_bytes=64)
                engine.tensor_tensor(
                    out=kept,
                    in0=gated[g],
                    in1=mask_kt[:, n].unsqueeze(1).to_broadcast([P, 2, P, PACK]),
                    op=ALU.mult,
                )
                masked[g] = kept

            def quantise_group(g):
                s, n, w = groups[g]
                kept = masked[g].rearrange("p e r t -> p (e r t)")
                if s == 1:
                    pair = slice(2 * w, 2 * w + 2)
                    nc.vector.quantize_mx(
                        out=left_codes[:, n, pair].rearrange("p c r -> p (c r)").bitcast(FP8X4),
                        scales=left_scales[:, n, pair].rearrange("p c r -> p (c r)"),
                        in_=kept,
                    )
                    return
                rows = slice(n * P, (n + 1) * P)
                for e in range(2):
                    nc.vector.quantize_mx(
                        out=right_codes[:, 2 * w + e, rows].bitcast(FP8X4),
                        scales=right_scales[:, 2 * w + e, rows],
                        in_=kept[:, e * RES : (e + 1) * RES],
                    )

            def quantise_tile(first):
                for g in range(first, first + PAIRS):
                    quantise_group(g)

            load_rows(0)
            for g in range(SIG_LEAD):
                sigmoid_group(g)
            for g in range(LEAD):
                transposed[g] = transposed_pair(0, g)
            transpose_mask(0)

            for turn in range(2 * TILES):
                if turn == 2:
                    nc.sync.dma_start(out=gain_bf16, in_=ln_c_g.partition_broadcast(P))
                    nc.sync.dma_start(out=bias_bf16, in_=ln_c_b.partition_broadcast(P))
                if turn == TILES:
                    nc.vector.tensor_copy(out=gain, in_=gain_bf16)
                    nc.vector.tensor_copy(out=bias, in_=bias_bf16)
                first = turn * PAIRS
                a = turn - TILES - 2
                for w in range(PAIRS):
                    g = first + w
                    if g + LEAD < len(groups):
                        prepare_projection(g + LEAD)
                    if g + SIG_LEAD < len(groups):
                        prepare_sigmoid(g + SIG_LEAD)
                    if a >= 0 and 0 < w < 3:
                        mean_passes(a, 4 * w - 4, 4 * w)
                    gate_group(g)
                    if g == PAIRS // 2 - 1:
                        mask_group(0)
                        mask_group(1)
                for g in (first, first + 2, first + 3, first + 1) if turn == 6 else range(first, first + PAIRS):
                    if turn > 0 or g >= PAIRS // 2:
                        mask_group(g)
                if turn >= 1:
                    quantise_tile(first - PAIRS)
                if a == 0:
                    centre_rows(0, norm)
                if a == 1:
                    nc.scalar.activation(out=warm, in_=eps, func=ACT.Abs_reciprocal_sqrt)
                    centre_rows(1, norm, lambda n: variance_step(0, n))
            mean_passes(2, 0, 8)
            quantise_tile(len(groups) - PAIRS)
            for h in range(2):
                rstd_half(0, h)

        with tc.tile_pool(name="late", bufs=2) as late:

            def normalise(a, start, width):
                centred = planes[a]
                cols = slice(start, start + width)
                nc.vector.tensor_tensor(
                    out=centred[:, :, cols],
                    in0=centred[:, :, cols],
                    in1=rstds[(a, start // HALF)][:, start % HALF : start % HALF + width].unsqueeze(1).to_broadcast([P, CH, width]),
                    op=ALU.mult,
                )

            def scale_shift(a, start, width, on_vector=0, on_scalar=0):
                centred = planes[a]
                cols = slice(start, start + width)
                for c in range(CH):
                    if c >= CH - on_scalar:
                        nc.scalar.activation(
                            out=centred[:, c, cols],
                            in_=centred[:, c, cols],
                            func=ACT.Identity,
                            scale=gain[:, c : c + 1],
                            bias=bias[:, c : c + 1],
                        )
                        continue
                    engine = nc.vector if c < on_vector else nc.gpsimd
                    engine.tensor_scalar(
                        out=centred[:, c, cols],
                        in0=centred[:, c, cols],
                        scalar1=gain[:, c : c + 1],
                        scalar2=bias[:, c : c + 1],
                        op0=ALU.mult,
                        op1=ALU.add,
                    )

            def store(a, start, width, on_vector=0):
                centred = planes[a]
                cols = slice(start, start + width)
                result = late.tile([P, HALF, CH], F32, tag="result", bufs=4)
                for n, q in enumerate(range(0, CH, QUAD)):
                    copy = nc.vector.tensor_copy if n < on_vector else nc.scalar.copy
                    copy(
                        out=result[:, :width, q : q + QUAD],
                        in_=centred[:, q : q + QUAD, cols].rearrange("p c j -> p j c"),
                    )
                nc.sync.dma_start(
                    out=out[a * P : (a + 1) * P, cols, :].rearrange("i j c -> i (j c)"),
                    in_=result[:, :width].rearrange("p j c -> p (j c)"),
                )

            normalise(0, 0, HALF)
            scale_shift(0, 0, HALF, 0)
            centre_rows(2, late, lambda n: variance_step(1, n))
            mean_passes(3, 0, 8)
            rstd_half(1, 0)
            rstd_half(1, 1)
            normalise(0, HALF, HALF)
            scale_shift(0, HALF, HALF, 0)
            store(0, 0, HALF, 0)
            normalise(1, 0, HALF)
            scale_shift(1, 0, HALF, 0)
            centre_rows(3, late, lambda n: variance_step(2, n))
            store(0, HALF, HALF, 0)
            rstd_half(2, 0)
            rstd_half(2, 1)
            normalise(1, HALF, HALF)
            scale_shift(1, HALF, HALF, 0)
            variance_half(3, 0)
            variance_half(3, 1)
            store(1, 0, HALF, 0)
            deviation_half(3, 0)
            rstd_half(3, 0)
            normalise(2, 0, HALF)
            deviation_half(3, 1)
            rstd_half(3, 1)
            normalise(2, HALF, HALF)
            scale_shift(2, 0, HALF, 8)
            scale_shift(2, HALF, HALF, 8)
            store(1, HALF, HALF, 1)
            store(2, 0, HALF, 0)
            normalise(3, 0, HALF)
            scale_shift(3, 0, HALF, 8)
            store(2, HALF, HALF, 1)
            store(3, 0, HALF, 1)
            normalise(3, HALF, HALF // 2)
            scale_shift(3, HALF, HALF // 2, 8)
            store(3, HALF, HALF // 2, 1)
            normalise(3, HALF + HALF // 2, HALF // 2)
            scale_shift(3, HALF + HALF // 2, HALF // 2, 8)
            store(3, HALF + HALF // 2, HALF // 2, 1)
